import numpy as np
import ml_dtypes


def mxq(x, axis, fmt="e4m3"):
    dtype, down = {"e4m3": (ml_dtypes.float8_e4m3fn, 7), "e5m2": (ml_dtypes.float8_e5m2, 14)}[fmt]
    v = np.moveaxis(np.asarray(x, np.float32).astype(ml_dtypes.bfloat16).astype(np.float64), axis, -1)
    blocks = v.reshape(v.shape[:-1] + (-1, 32))
    amax = np.abs(blocks).max(-1, keepdims=True)
    byte = np.maximum(np.where(amax > 0, np.frexp(amax)[1] - 1 + 127, 0) - down, 1)
    scale = np.exp2(byte - 127.0)
    codes = (blocks / scale).astype(np.float32).astype(dtype).astype(np.float64)
    return np.moveaxis((codes * scale).reshape(v.shape), -1, axis)


WIDE = False


def mx_kscale(k):
    if not WIDE:
        return np.ones(k)
    levels = np.array([10, -10, 5, -5, 0])
    if k % 512:
        return np.exp2(np.random.permutation(np.resize(levels, k // 32))).repeat(32)
    a = np.empty((k // 512, 16))
    for p in range(k // 512):
        a[p, :8] = np.random.permutation(np.resize(levels, 8))
        for g in range(8):
            far = levels[np.abs(levels - a[p, g]) >= 10]
            a[p, g + 8] = far[np.random.randint(len(far))]
    return np.exp2(a.ravel()).repeat(32)


BF16 = ml_dtypes.bfloat16


def bf(x):
    return np.asarray(x, np.float32).astype(BF16)


def f64(x):
    return np.asarray(x).astype(np.float64)


B, O, D, G1, G2, F1, F2 = 256, 8, 1024, 1024, 1024, 1024, 1024
C = D + D
P = O * O


def setup_inputs():
    s = mx_kscale(C)[:D]
    ss = np.concatenate([s, s])
    t = mx_kscale(G1)
    return {
        "objs": bf(np.random.standard_normal((B, O, D)) * s),
        "W1": bf(np.random.standard_normal((G1, C)) / np.sqrt(C) / ss * t[:, None]),
        "b1": bf(np.random.standard_normal(G1) * 0.3 * t),
        "W2": bf(np.random.standard_normal((G2, G1)) * 0.5 / np.sqrt(G1) / t),
        "b2": bf(np.random.standard_normal(G2) * 0.15),
    }


def reference(objs, W1, b1, W2, b2):
    v = f64(objs)
    v_i = np.broadcast_to(v[:, None, :, :], (B, O, O, D))
    v_j = np.broadcast_to(v[:, :, None, :], (B, O, O, D))
    pairs = np.concatenate([v_i, v_j], axis=-1).reshape(B, P, C)
    h = np.maximum((mxq(pairs, 2, "e4m3") @ mxq(f64(W1).T, 0, "e4m3")) + f64(b1), 0.0)
    x_pairs = np.maximum((mxq(h, 2, "e4m3") @ mxq(f64(W2).T, 0, "e4m3")) + f64(b2), 0.0)
    return x_pairs, x_pairs.sum(axis=1)

@@ -1,0 +1,285 @@
+from contextlib import ExitStack
+
+import concourse.mybir as mybir
+from concourse.masks import make_identity
+
+F32 = mybir.dt.float32
+BF16 = mybir.dt.bfloat16
+U32 = mybir.dt.uint32
+U8 = mybir.dt.uint8
+FP8X4 = mybir.dt.float8_e4m3fn_x4
+ACT = mybir.ActivationFunctionType
+ALU = mybir.AluOpType
+
+P = 128
+SETS, OBJ, D = 256, 8, 1024
+HID, OUTC = 1024, 1024
+FLOPS = 2 * (SETS * OBJ) * (2 * D) * HID + 2 * (SETS * OBJ * OBJ) * HID * OUTC
+
+
+def tile_pairwiserelationmodule_pa_l_kernel(tc, objs, W1, b1, W2, b2, out_0, out_1):
+    nc = tc.nc
+    xp_rows = out_0.flatten_outer_dims()
+
+    with ExitStack() as ctx:
+        const = ctx.enter_context(tc.tile_pool(name="const", bufs=1))
+        big = ctx.enter_context(tc.tile_pool(name="big", bufs=4))
+        mid = ctx.enter_context(tc.tile_pool(name="mid", bufs=3))
+        abp = ctx.enter_context(tc.tile_pool(name="abp", bufs=2))
+        cod = ctx.enter_context(tc.tile_pool(name="cod", bufs=3))
+        xsp = ctx.enter_context(tc.tile_pool(name="xsp", bufs=6))
+        psum = ctx.enter_context(tc.psum_pool(name="psum", bufs=2))
+
+        PS_BUFS = {"y": 3, "tr": 3, "s1": 2}
+        HEAD_TAGS = ["tr", "y", "s1", "tr", "y", "s1", "tr", "y"]
+        state = {"head": 0, "evac": 0}
+
+        def psum_tile(shape, tag, name):
+            return psum.tile(shape, F32, tag=tag, bufs=PS_BUFS[tag], name=name)
+
+        def head_psum(in_head):
+            tag = "tr"
+            if in_head:
+                tag = HEAD_TAGS[state["head"] % 8]
+                state["head"] = state["head"] + 1
+            return psum_tile([P, 2, 2, P], tag, "pt")
+
+        def word_copy(out, in_):
+            if state["evac"] % 2 == 0:
+                nc.vector.tensor_copy(out=out, in_=in_)
+            else:
+                nc.scalar.copy(out=out, in_=in_)
+            state["evac"] = state["evac"] + 1
+
+        ident = const.tile([P, P], F32, name="ident")
+        make_identity(nc, ident[:])
+
+        w1c = const.tile([P, 4, HID], U32, name="w1c", align_bytes=64)
+        w1s = const.tile([P, 4, HID], U8, name="w1s", align_bytes=64)
+        w2c = const.tile([P, 2, OUTC], U32, name="w2c", align_bytes=64)
+        w2s = const.tile([P, 2, OUTC], U8, name="w2s", align_bytes=64)
+        oc = const.tile([P, 2, 2, 1024], U32, name="oc", align_bytes=64)
+        osc = const.tile([P, 2, 2, 1024], U8, name="osc", align_bytes=64)
+        sT = const.tile([P, 8, SETS], F32, name="sT")
+        b1t = const.tile([P, 2, 4], F32, name="b1t")
+        b2t = const.tile([P, 8], F32, name="b2t")
+
+        oraw = []
+        for hf in range(2):
+            oraw_t = big.tile([P, OBJ, D], BF16, tag="big16", name="oraw")
+            oraw.append(oraw_t)
+        w1raw = []
+        for g in range(2):
+            w1raw_t = big.tile([P, 4, 2 * D], BF16, tag="big16", name="w1raw")
+            w1raw.append(w1raw_t)
+
+        zall = const.tile([P, 512], BF16, name="zall")
+        nc.vector.memset(zall[:], 0.0)
+        nc.sync.dma_start(out=zall[0:2, :], in_=b1.rearrange("(g x) -> g x", g=2))
+        nc.sync.dma_start(out=zall[2:4, :], in_=b2.rearrange("(g x) -> g x", g=2))
+        nc.sync.dma_start(out=oraw[0][:], in_=objs[0:P])
+        for g in range(2):
+            nc.sync.dma_start(
+                out=w1raw[g][:],
+                in_=W1[512 * g : 512 * (g + 1), :].rearrange("(m t) k -> m t k", t=4),
+            )
+        nc.sync.dma_start(out=oraw[1][:], in_=objs[P : 2 * P])
+
+        zf = const.tile([P, 512], F32, name="zf")
+        nc.vector.tensor_copy(out=zf[:], in_=zall[:])
+        pb1 = psum_tile([P, 4, P], "s1", "pb1")
+        for t in range(4):
+            nc.tensor.transpose(pb1[:, t, :], zf[:, t:512:4], ident[:])
+        nc.vector.tensor_copy(out=b1t[:], in_=pb1[:, :, 0:2].rearrange("p t g -> p g t"))
+        pb2 = psum_tile([P, 4, P], "s1", "pb2")
+        for jj in range(4):
+            nc.tensor.transpose(pb2[:, jj, :], zf[:, jj * P : (jj + 1) * P], ident[:])
+        nc.vector.tensor_copy(
+            out=b2t[:].rearrange("p (r j) -> p r j", r=2),
+            in_=pb2[:, :, 2:4].rearrange("p j r -> p r j"),
+        )
+
+        def turn_pair(words, base0, base1, in_head):
+            pt = head_psum(in_head)
+            for s, base in enumerate((base0, base1)):
+                for u in range(2):
+                    nc.tensor.transpose(pt[:, s, u, :], words[:, base + u : base + 256 : 2], ident[:])
+            return pt
+
+        def prep_objs(hf, in_head):
+            words = oraw[hf][:].rearrange("p o d -> p (o d)").bitcast(F32)
+            for kk in range(2):
+                grp = mid.tile([P, 1024, 4], BF16, tag="mid8", name="grp", align_bytes=64)
+                flat = grp[:].rearrange("p c j -> p (c j)")
+                gw = flat.bitcast(F32).rearrange("p (h o l u) -> p h o l u", h=8, o=8, l=16)
+                for op in range(4):
+                    pt = turn_pair(words, (2 * op) * 512 + 256 * kk, (2 * op + 1) * 512 + 256 * kk, in_head)
+                    for s in range(2):
+                        word_copy(
+                            gw[:, :, 2 * op + s, :, :],
+                            pt[:, s, :, :].rearrange("p u (h l) -> p h l u", h=8),
+                        )
+                nc.vector.quantize_mx(out=oc[:, hf, kk, :].bitcast(FP8X4), scales=osc[:, hf, kk, :], in_=flat)
+
+        def prep_weights(raws, slots_per_raw, words_per_slot, passes, codes, scales):
+            views = [r[:].rearrange("p s k -> p (s k)").bitcast(F32) for r in raws]
+            for kk in range(passes):
+                grp = mid.tile([P, 1024, 4], BF16, tag="mid8", name="grp", align_bytes=64)
+                flat = grp[:].rearrange("p c j -> p (c j)")
+                gw = flat.bitcast(F32)
+                col = 0
+                for words in views:
+                    for sp in range(slots_per_raw // 2):
+                        pt = turn_pair(
+                            words,
+                            (2 * sp) * words_per_slot + 256 * kk,
+                            (2 * sp + 1) * words_per_slot + 256 * kk,
+                            True,
+                        )
+                        word_copy(
+                            gw[:, 2 * col : 2 * (col + 256)].rearrange("p (s r u) -> p s r u", s=2, u=2),
+                            pt[:].rearrange("p s u r -> p s r u"),
+                        )
+                        col += 256
+                nc.vector.quantize_mx(out=codes[:, kk, :].bitcast(FP8X4), scales=scales[:, kk, :], in_=flat)
+
+        ab = {}
+        hq = {}
+        xts = {}
+
+        def stage1(u):
+            hf, bh = divmod(u, 8)
+            cols = slice(bh * P, (bh + 1) * P)
+            at = abp.tile([P, 2, P, 4], F32, tag="at", name="at")
+            bt = abp.tile([P, 2, P, 4], F32, tag="bt", name="bt")
+            for part in range(2):
+                for g in range(2):
+                    ps = psum_tile([P, 4, P], "s1", "ps1")
+                    for t in range(4):
+                        wcol = slice((g * 4 + t) * P, (g * 4 + t + 1) * P)
+                        for kk in range(2):
+                            nc.tensor.matmul_mx(
+                                out=ps[:, t, :],
+                                lhsT=w1c[:, 2 * part + kk, wcol].bitcast(FP8X4),
+                                lhsT_scale=w1s[:, 2 * part + kk, wcol],
+                                rhs=oc[:, hf, kk, cols].bitcast(FP8X4),
+                                rhs_scale=osc[:, hf, kk, cols],
+                                start=(kk == 0),
+                                stop=(kk == 1),
+                            )
+                    src = ps[:].rearrange("p t c -> p c t")
+                    if part == 0:
+                        nc.vector.tensor_tensor(
+                            out=at[:, g],
+                            in0=src,
+                            in1=b1t[:, g, :].unsqueeze(1).to_broadcast([P, P, 4]),
+                            op=ALU.add,
+                        )
+                    else:
+                        nc.scalar.copy(out=bt[:, g], in_=src)
+            ab[u] = (at, bt)
+
+        def hform(i):
+            u, beta = divmod(i, 2)
+            at, bt = ab[u]
+            hb = mid.tile([P, 2, 512, 4], BF16, tag="mid8", name="hb", align_bytes=64)
+            lo = slice(beta * 32, (beta + 1) * 32)
+            for g in range(2):
+                nc.vector.tensor_tensor(
+                    out=hb[:, g].rearrange("p (k m b) t -> p k m (b t)", k=8, m=8),
+                    in0=at[:, g].rearrange("p (o l) t -> p o (l t)", o=8)[:, :, lo].unsqueeze(1).to_broadcast([P, 8, 8, 32]),
+                    in1=bt[:, g].rearrange("p (o l) t -> p o (l t)", o=8)[:, :, lo].unsqueeze(2).to_broadcast([P, 8, 8, 32]),
+                    op=ALU.add,
+                )
+            flat = hb[:].rearrange("p g c t -> p (g c t)")
+            nc.vector.tensor_scalar_max(out=flat, in0=flat, scalar1=0.0)
+            hc = cod.tile([P, 1024], U32, tag="hc", name="hc", align_bytes=64)
+            hs = cod.tile([P, 1024], U8, tag="hs", name="hs", align_bytes=64)
+            nc.vector.quantize_mx(out=hc[:].bitcast(FP8X4), scales=hs[:], in_=flat)
+            hq[i] = (hc, hs)
+
+        def stage2(i):
+            hc, hs = hq[i]
+            xT = big.tile([P, 8, 8, 64], F32, tag="big16", name="xT")
+            for j in range(8):
+                y = psum_tile([P, 512], "y", "y")
+                wcol = slice(j * P, (j + 1) * P)
+                for g in range(2):
+                    tok = slice(g * 512, (g + 1) * 512)
+                    nc.tensor.matmul_mx(
+                        out=y[:],
+                        lhsT=w2c[:, g, wcol].bitcast(FP8X4),
+                        lhsT_scale=w2s[:, g, wcol],
+                        rhs=hc[:, tok].bitcast(FP8X4),
+                        rhs_scale=hs[:, tok],
+                        start=(g == 0),
+                        stop=(g == 1),
+                    )
+                yv = y[:].rearrange("p (q b) -> p b q", b=8)
+                for b in range(8):
+                    nc.scalar.activation(
+                        out=xT[:, j, b, :],
+                        in_=yv[:, b, :],
+                        func=ACT.Relu,
+                        bias=b2t[:, j : j + 1],
+                        scale=1.0,
+                        accum_out=sT[:, j, 8 * i + b : 8 * i + b + 1],
+                    )
+            xts[i] = xT
+
+        def turn_back(i):
+            xT = xts[i]
+            for sb in range(4):
+                xs = xsp.tile([P, OUTC], F32, tag="xs", name="xs")
+                for hh in range(2):
+                    tb = psum_tile([P, 512], "tr", "tb")
+                    for jj in range(4):
+                        nc.tensor.transpose(
+                            tb[:, jj * P : (jj + 1) * P],
+                            xT[:, hh * 4 + jj, 2 * sb : 2 * sb + 2, :].rearrange("p b q -> p (b q)"),
+                            ident[:],
+                        )
+                    if hh == 0:
+                        nc.vector.tensor_copy(out=xs[:, 0:512], in_=tb[:])
+                    else:
+                        nc.scalar.copy(out=xs[:, 512:1024], in_=tb[:])
+                row = (8 * i + 2 * sb) * 64
+                nc.sync.dma_start(out=xp_rows[row : row + P, :], in_=xs[:])
+
+        def sums_out(hf):
+            so = xsp.tile([P, OUTC], F32, tag="xs", name="so")
+            for hh in range(2):
+                tb = psum_tile([P, 512], "tr", "tbs")
+                for jj in range(4):
+                    nc.tensor.transpose(
+                        tb[:, jj * P : (jj + 1) * P],
+                        sT[:, hh * 4 + jj, hf * P : (hf + 1) * P],
+                        ident[:],
+                    )
+                if hh == 0:
+                    nc.vector.tensor_copy(out=so[:, 0:512], in_=tb[:])
+                else:
+                    nc.scalar.copy(out=so[:, 512:1024], in_=tb[:])
+            nc.sync.dma_start(out=out_1[hf * P : (hf + 1) * P, :], in_=so[:])
+
+        prep_objs(0, True)
+        prep_weights(w1raw, 4, 1024, 4, w1c, w1s)
+        w2raw = big.tile([P, 8, HID], BF16, tag="big16", name="w2raw")
+        nc.sync.dma_start(out=w2raw[:], in_=W2.rearrange("(j m) g -> m j g", m=P))
+        stage1(0)
+        prep_weights([w2raw], 8, 512, 2, w2c, w2s)
+        hform(0)
+        for i in range(32):
+            if i % 2 == 1 and (i + 1) // 2 < 16:
+                stage1((i + 1) // 2)
+            if i + 1 < 32:
+                hform(i + 1)
+            stage2(i)
+            if i >= 1:
+                turn_back(i - 1)
+            if i == 1:
+                prep_objs(1, False)
+            if i == 17:
+                sums_out(0)
+        turn_back(31)
+        sums_out(1)

@@ -15,24 +15,30 @@ P = 128
 SETS, OBJ, D = 256, 8, 1024
 HID, OUTC = 1024, 1024
 FLOPS = 2 * (SETS * OBJ) * (2 * D) * HID + 2 * (SETS * OBJ * OBJ) * HID * OUTC
+N_BLOCKS = 32
+N_UNITS = 16
 
 
 def tile_pairwiserelationmodule_pa_l_kernel(tc, objs, W1, b1, W2, b2, out_0, out_1):
     nc = tc.nc
     xp_rows = out_0.flatten_outer_dims()
+    obj_rows = objs.flatten_outer_dims()
 
     with ExitStack() as ctx:
         const = ctx.enter_context(tc.tile_pool(name="const", bufs=1))
-        big = ctx.enter_context(tc.tile_pool(name="big", bufs=4))
+        r8 = ctx.enter_context(tc.tile_pool(name="r8", bufs=6))
         mid = ctx.enter_context(tc.tile_pool(name="mid", bufs=3))
+        xvp = ctx.enter_context(tc.tile_pool(name="xvp", bufs=2))
+        ocp = ctx.enter_context(tc.tile_pool(name="ocp", bufs=2))
         abp = ctx.enter_context(tc.tile_pool(name="abp", bufs=2))
-        cod = ctx.enter_context(tc.tile_pool(name="cod", bufs=3))
-        xsp = ctx.enter_context(tc.tile_pool(name="xsp", bufs=6))
+        cod = ctx.enter_context(tc.tile_pool(name="cod", bufs=4))
+        xsp = ctx.enter_context(tc.tile_pool(name="xsp", bufs=4))
         psum = ctx.enter_context(tc.psum_pool(name="psum", bufs=2))
+        ctx.enter_context(tc.manual_schedule())
 
-        PS_BUFS = {"y": 3, "tr": 3, "s1": 2}
-        HEAD_TAGS = ["tr", "y", "s1", "tr", "y", "s1", "tr", "y"]
-        state = {"head": 0, "evac": 0}
+        PS_BUFS = {"y": 4, "tr": 2, "s1": 2}
+        HEAD_TAGS = ["y", "y", "tr", "y", "y", "tr"]
+        state = {"head": 0}
 
         def psum_tile(shape, tag, name):
             return psum.tile(shape, F32, tag=tag, bufs=PS_BUFS[tag], name=name)
@@ -40,16 +46,15 @@ def tile_pairwiserelationmodule_pa_l_kernel(tc, objs, W1, b1, W2, b2, out_0, out
         def head_psum(in_head):
             tag = "tr"
             if in_head:
-                tag = HEAD_TAGS[state["head"] % 8]
+                tag = HEAD_TAGS[state["head"] % 6]
                 state["head"] = state["head"] + 1
             return psum_tile([P, 2, 2, P], tag, "pt")
 
-        def word_copy(out, in_):
-            if state["evac"] % 2 == 0:
+        def word_copy(engine, out, in_):
+            if engine == "v":
                 nc.vector.tensor_copy(out=out, in_=in_)
             else:
                 nc.scalar.copy(out=out, in_=in_)
-            state["evac"] = state["evac"] + 1
 
         ident = const.tile([P, P], F32, name="ident")
         make_identity(nc, ident[:])
@@ -58,193 +63,227 @@ def tile_pairwiserelationmodule_pa_l_kernel(tc, objs, W1, b1, W2, b2, out_0, out
         w1s = const.tile([P, 4, HID], U8, name="w1s", align_bytes=64)
         w2c = const.tile([P, 2, OUTC], U32, name="w2c", align_bytes=64)
         w2s = const.tile([P, 2, OUTC], U8, name="w2s", align_bytes=64)
-        oc = const.tile([P, 2, 2, 1024], U32, name="oc", align_bytes=64)
-        osc = const.tile([P, 2, 2, 1024], U8, name="osc", align_bytes=64)
         sT = const.tile([P, 8, SETS], F32, name="sT")
         b1t = const.tile([P, 2, 4], F32, name="b1t")
         b2t = const.tile([P, 8], F32, name="b2t")
+        zall = const.tile([P, 640], BF16, name="zall")
+        zf = const.tile([P, 640], F32, name="zf")
 
-        oraw = []
-        for hf in range(2):
-            oraw_t = big.tile([P, OBJ, D], BF16, tag="big16", name="oraw")
-            oraw.append(oraw_t)
-        w1raw = []
-        for g in range(2):
-            w1raw_t = big.tile([P, 4, 2 * D], BF16, tag="big16", name="w1raw")
-            w1raw.append(w1raw_t)
+        def raw_tile():
+            return r8.tile([P, 8, 512], BF16, tag="r8", name="raw", align_bytes=64)
 
-        zall = const.tile([P, 512], BF16, name="zall")
-        nc.vector.memset(zall[:], 0.0)
-        nc.sync.dma_start(out=zall[0:2, :], in_=b1.rearrange("(g x) -> g x", g=2))
-        nc.sync.dma_start(out=zall[2:4, :], in_=b2.rearrange("(g x) -> g x", g=2))
-        nc.sync.dma_start(out=oraw[0][:], in_=objs[0:P])
-        for g in range(2):
+        def load_bias():
+            nc.vector.memset(zall[:], 0.0)
+            nc.sync.dma_start(out=zall[0:2, 0:512], in_=b1.rearrange("(g x) -> g x", g=2))
             nc.sync.dma_start(
-                out=w1raw[g][:],
-                in_=W1[512 * g : 512 * (g + 1), :].rearrange("(m t) k -> m t k", t=4),
+                out=zall[0:8, 512:640].rearrange("j (q b) -> j q b", q=4),
+                in_=b2.rearrange("(q j b) -> j q b", q=4, j=8),
             )
-        nc.sync.dma_start(out=oraw[1][:], in_=objs[P : 2 * P])
 
-        zf = const.tile([P, 512], F32, name="zf")
-        nc.vector.tensor_copy(out=zf[:], in_=zall[:])
-        pb1 = psum_tile([P, 4, P], "s1", "pb1")
-        for t in range(4):
-            nc.tensor.transpose(pb1[:, t, :], zf[:, t:512:4], ident[:])
-        nc.vector.tensor_copy(out=b1t[:], in_=pb1[:, :, 0:2].rearrange("p t g -> p g t"))
-        pb2 = psum_tile([P, 4, P], "s1", "pb2")
-        for jj in range(4):
-            nc.tensor.transpose(pb2[:, jj, :], zf[:, jj * P : (jj + 1) * P], ident[:])
-        nc.vector.tensor_copy(
-            out=b2t[:].rearrange("p (r j) -> p r j", r=2),
-            in_=pb2[:, :, 2:4].rearrange("p j r -> p r j"),
-        )
+        def load_objs(gq):
+            raw = raw_tile()
+            nc.sync.dma_start(
+                out=raw[:].rearrange("p (s k) d -> p s (k d)", k=2),
+                in_=obj_rows[512 * gq : 512 * (gq + 1), :].rearrange("(s p) d -> p s d", p=P),
+            )
+            return raw
 
-        def turn_pair(words, base0, base1, in_head):
+        def load_w1(kk):
+            raw = raw_tile()
+            for g in range(2):
+                nc.sync.dma_start(
+                    out=raw[:, 4 * g : 4 * g + 4, :],
+                    in_=W1[512 * g : 512 * (g + 1), 512 * kk : 512 * (kk + 1)].rearrange("(m t) k -> m t k", t=4),
+                )
+            return raw
+
+        def load_w2(kk):
+            raw = raw_tile()
+            nc.sync.dma_start(
+                out=raw[:],
+                in_=W2[:, 512 * kk : 512 * (kk + 1)].rearrange("(s m) g -> m s g", m=P),
+            )
+            return raw
+
+        def prep_bias():
+            nc.vector.tensor_copy(out=zf[:], in_=zall[:])
+            pb1 = psum_tile([P, 4, P], "s1", "pb1")
+            for t in range(4):
+                nc.tensor.transpose(pb1[:, t, :], zf[:, t:512:4], ident[:])
+            nc.vector.tensor_copy(out=b1t[:], in_=pb1[:, :, 0:2].rearrange("p t g -> p g t"))
+            pb2 = psum_tile([P, 4, P], "s1", "pb2")
+            nc.tensor.transpose(pb2[:, 0, :], zf[:, 512:640], ident[:])
+            nc.vector.tensor_copy(out=b2t[:], in_=pb2[:, 0, 0:8])
+
+        def turn_pair(raw, s0, in_head):
+            words = raw[:].rearrange("p s k -> p (s k)").bitcast(F32)
             pt = head_psum(in_head)
-            for s, base in enumerate((base0, base1)):
+            for s in range(2):
                 for u in range(2):
+                    base = (s0 + s) * 256
                     nc.tensor.transpose(pt[:, s, u, :], words[:, base + u : base + 256 : 2], ident[:])
             return pt
 
-        def prep_objs(hf, in_head):
-            words = oraw[hf][:].rearrange("p o d -> p (o d)").bitcast(F32)
-            for kk in range(2):
-                grp = mid.tile([P, 1024, 4], BF16, tag="mid8", name="grp", align_bytes=64)
-                flat = grp[:].rearrange("p c j -> p (c j)")
-                gw = flat.bitcast(F32).rearrange("p (h o l u) -> p h o l u", h=8, o=8, l=16)
-                for op in range(4):
-                    pt = turn_pair(words, (2 * op) * 512 + 256 * kk, (2 * op + 1) * 512 + 256 * kk, in_head)
-                    for s in range(2):
-                        word_copy(
-                            gw[:, :, 2 * op + s, :, :],
-                            pt[:, s, :, :].rearrange("p u (h l) -> p h l u", h=8),
-                        )
-                nc.vector.quantize_mx(out=oc[:, hf, kk, :].bitcast(FP8X4), scales=osc[:, hf, kk, :], in_=flat)
+        def grp_tile():
+            return mid.tile([P, 1024, 4], BF16, tag="mid8", name="grp", align_bytes=64)
 
-        def prep_weights(raws, slots_per_raw, words_per_slot, passes, codes, scales):
-            views = [r[:].rearrange("p s k -> p (s k)").bitcast(F32) for r in raws]
-            for kk in range(passes):
-                grp = mid.tile([P, 1024, 4], BF16, tag="mid8", name="grp", align_bytes=64)
-                flat = grp[:].rearrange("p c j -> p (c j)")
-                gw = flat.bitcast(F32)
-                col = 0
-                for words in views:
-                    for sp in range(slots_per_raw // 2):
-                        pt = turn_pair(
-                            words,
-                            (2 * sp) * words_per_slot + 256 * kk,
-                            (2 * sp + 1) * words_per_slot + 256 * kk,
-                            True,
-                        )
-                        word_copy(
-                            gw[:, 2 * col : 2 * (col + 256)].rearrange("p (s r u) -> p s r u", s=2, u=2),
-                            pt[:].rearrange("p s u r -> p s r u"),
-                        )
-                        col += 256
-                nc.vector.quantize_mx(out=codes[:, kk, :].bitcast(FP8X4), scales=scales[:, kk, :], in_=flat)
+        def plain_bank(raw, grp, sp, engine, in_head):
+            gw = grp[:].rearrange("p c j -> p (c j)").bitcast(F32)
+            pt = turn_pair(raw, 2 * sp, in_head)
+            word_copy(
+                engine,
+                gw[:, 512 * sp : 512 * (sp + 1)].rearrange("p (s r u) -> p s r u", s=2, u=2),
+                pt[:].rearrange("p s u r -> p s r u"),
+            )
 
+        def w2_bank(raw, grp, sp, engine):
+            gw = grp[:].rearrange("p c j -> p (c j)").bitcast(F32).rearrange(
+                "p (j q b u) -> p j q b u", j=8, q=4, b=32
+            )
+            pt = turn_pair(raw, 2 * sp, True)
+            for sl in range(2):
+                word_copy(
+                    engine,
+                    gw[:, 4 * sl : 4 * sl + 4, sp, :, :],
+                    pt[:, sl, :, :].rearrange("p u (j b) -> p j b u", j=4),
+                )
+
+        def quant(grp, codes, scales):
+            nc.vector.quantize_mx(
+                out=codes.bitcast(FP8X4), scales=scales, in_=grp[:].rearrange("p c j -> p (c j)")
+            )
+
+        ocs = {}
         ab = {}
+        hbs = {}
         hq = {}
         xts = {}
 
-        def stage1(u):
-            hf, bh = divmod(u, 8)
-            cols = slice(bh * P, (bh + 1) * P)
-            at = abp.tile([P, 2, P, 4], F32, tag="at", name="at")
-            bt = abp.tile([P, 2, P, 4], F32, tag="bt", name="bt")
-            for part in range(2):
-                for g in range(2):
-                    ps = psum_tile([P, 4, P], "s1", "ps1")
-                    for t in range(4):
-                        wcol = slice((g * 4 + t) * P, (g * 4 + t + 1) * P)
-                        for kk in range(2):
-                            nc.tensor.matmul_mx(
-                                out=ps[:, t, :],
-                                lhsT=w1c[:, 2 * part + kk, wcol].bitcast(FP8X4),
-                                lhsT_scale=w1s[:, 2 * part + kk, wcol],
-                                rhs=oc[:, hf, kk, cols].bitcast(FP8X4),
-                                rhs_scale=osc[:, hf, kk, cols],
-                                start=(kk == 0),
-                                stop=(kk == 1),
-                            )
-                    src = ps[:].rearrange("p t c -> p c t")
-                    if part == 0:
-                        nc.vector.tensor_tensor(
-                            out=at[:, g],
-                            in0=src,
-                            in1=b1t[:, g, :].unsqueeze(1).to_broadcast([P, P, 4]),
-                            op=ALU.add,
+        def stage1_half(u, part):
+            oc, osc = ocs[u // 4]
+            dst = abp.tile([P, 2, P, 4], F32, tag="at" if part == 0 else "bt", name="abt")
+            for g in range(2):
+                ps = psum_tile([P, 4, P], "s1", "ps1")
+                for t in range(4):
+                    wcol = slice((g * 4 + t) * P, (g * 4 + t + 1) * P)
+                    for kk in range(2):
+                        nc.tensor.matmul_mx(
+                            out=ps[:, t, :],
+                            lhsT=w1c[:, 2 * part + kk, wcol].bitcast(FP8X4),
+                            lhsT_scale=w1s[:, 2 * part + kk, wcol],
+                            rhs=oc[:, u % 4, kk, :].bitcast(FP8X4),
+                            rhs_scale=osc[:, u % 4, kk, :],
+                            start=(kk == 0),
+                            stop=(kk == 1),
                         )
-                    else:
-                        nc.scalar.copy(out=bt[:, g], in_=src)
-            ab[u] = (at, bt)
+                src = ps[:].rearrange("p t c -> p c t")
+                if part == 0:
+                    nc.vector.tensor_tensor(
+                        out=dst[:, g],
+                        in0=src,
+                        in1=b1t[:, g, :].unsqueeze(1).to_broadcast([P, P, 4]),
+                        op=ALU.add,
+                    )
+                else:
+                    nc.scalar.copy(out=dst[:, g], in_=src)
+            ab[(u, part)] = dst
 
-        def hform(i):
+        def h_add(i):
             u, beta = divmod(i, 2)
-            at, bt = ab[u]
+            at = ab[(u, 0)]
+            bt = ab[(u, 1)]
             hb = mid.tile([P, 2, 512, 4], BF16, tag="mid8", name="hb", align_bytes=64)
-            lo = slice(beta * 32, (beta + 1) * 32)
+            cols = slice(beta * 64, (beta + 1) * 64)
             for g in range(2):
                 nc.vector.tensor_tensor(
-                    out=hb[:, g].rearrange("p (k m b) t -> p k m (b t)", k=8, m=8),
-                    in0=at[:, g].rearrange("p (o l) t -> p o (l t)", o=8)[:, :, lo].unsqueeze(1).to_broadcast([P, 8, 8, 32]),
-                    in1=bt[:, g].rearrange("p (o l) t -> p o (l t)", o=8)[:, :, lo].unsqueeze(2).to_broadcast([P, 8, 8, 32]),
+                    out=hb[:, g].rearrange("p (b k m) t -> p b k m t", b=8, k=8),
+                    in0=at[:, g, cols, :].rearrange("p (b m) t -> p b m t", b=8).unsqueeze(2).to_broadcast([P, 8, 8, 8, 4]),
+                    in1=bt[:, g, cols, :].rearrange("p (b k) t -> p b k t", b=8).unsqueeze(3).to_broadcast([P, 8, 8, 8, 4]),
                     op=ALU.add,
                 )
-            flat = hb[:].rearrange("p g c t -> p (g c t)")
-            nc.vector.tensor_scalar_max(out=flat, in0=flat, scalar1=0.0)
+            hbs[i] = hb
+
+        def h_relu(i):
+            for g in range(2):
+                flat = hbs[i][:, g].rearrange("p c t -> p (c t)")
+                nc.vector.tensor_scalar_max(out=flat, in0=flat, scalar1=0.0)
+
+        def h_quant(i):
             hc = cod.tile([P, 1024], U32, tag="hc", name="hc", align_bytes=64)
             hs = cod.tile([P, 1024], U8, tag="hs", name="hs", align_bytes=64)
-            nc.vector.quantize_mx(out=hc[:].bitcast(FP8X4), scales=hs[:], in_=flat)
+            nc.vector.quantize_mx(
+                out=hc[:].bitcast(FP8X4), scales=hs[:], in_=hbs[i][:].rearrange("p g c t -> p (g c t)")
+            )
             hq[i] = (hc, hs)
 
-        def stage2(i):
-            hc, hs = hq[i]
-            xT = big.tile([P, 8, 8, 64], F32, tag="big16", name="xT")
-            for j in range(8):
-                y = psum_tile([P, 512], "y", "y")
-                wcol = slice(j * P, (j + 1) * P)
-                for g in range(2):
-                    tok = slice(g * 512, (g + 1) * 512)
-                    nc.tensor.matmul_mx(
-                        out=y[:],
-                        lhsT=w2c[:, g, wcol].bitcast(FP8X4),
-                        lhsT_scale=w2s[:, g, wcol],
-                        rhs=hc[:, tok].bitcast(FP8X4),
-                        rhs_scale=hs[:, tok],
-                        start=(g == 0),
-                        stop=(g == 1),
-                    )
-                yv = y[:].rearrange("p (q b) -> p b q", b=8)
-                for b in range(8):
-                    nc.scalar.activation(
-                        out=xT[:, j, b, :],
-                        in_=yv[:, b, :],
-                        func=ACT.Relu,
-                        bias=b2t[:, j : j + 1],
-                        scale=1.0,
-                        accum_out=sT[:, j, 8 * i + b : 8 * i + b + 1],
-                    )
-            xts[i] = xT
+        def stage2_open(i):
+            xv = xvp.tile([P, 8, 8, 32], F32, tag="xv", name="xv", align_bytes=64, bufs=3)
+            xp = xvp.tile([P, 8, 4, 64], F32, tag="xp", name="xp", align_bytes=64)
+            xts[i] = (xv, xp)
 
-        def turn_back(i):
-            xT = xts[i]
-            for sb in range(4):
-                xs = xsp.tile([P, OUTC], F32, tag="xs", name="xs")
-                for hh in range(2):
-                    tb = psum_tile([P, 512], "tr", "tb")
-                    for jj in range(4):
-                        nc.tensor.transpose(
-                            tb[:, jj * P : (jj + 1) * P],
-                            xT[:, hh * 4 + jj, 2 * sb : 2 * sb + 2, :].rearrange("p b q -> p (b q)"),
-                            ident[:],
-                        )
-                    if hh == 0:
-                        nc.vector.tensor_copy(out=xs[:, 0:512], in_=tb[:])
-                    else:
-                        nc.scalar.copy(out=xs[:, 512:1024], in_=tb[:])
-                row = (8 * i + 2 * sb) * 64
-                nc.sync.dma_start(out=xp_rows[row : row + P, :], in_=xs[:])
+        def stage2(i, j):
+            hc, hs = hq[i]
+            xv, xp = xts[i]
+            y = psum_tile([P, 512], "y", "y")
+            wcol = slice(j * P, (j + 1) * P)
+            for g in range(2):
+                tok = slice(g * 512, (g + 1) * 512)
+                nc.tensor.matmul_mx(
+                    out=y[:],
+                    lhsT=w2c[:, g, wcol].bitcast(FP8X4),
+                    lhsT_scale=w2s[:, g, wcol],
+                    rhs=hc[:, tok].bitcast(FP8X4),
+                    rhs_scale=hs[:, tok],
+                    start=(g == 0),
+                    stop=(g == 1),
+                )
+            for b in range(8):
+                src = y[:, 64 * b : 64 * (b + 1)]
+                if b < 4:
+                    dst = xv[:, 2 * b : 2 * b + 2, j, :]
+                    src = src.rearrange("p (s a) -> p s a", a=32)
+                else:
+                    dst = xp[:, j, b - 4, :]
+                nc.scalar.activation(
+                    out=dst,
+                    in_=src,
+                    func=ACT.Relu,
+                    bias=b2t[:, j : j + 1],
+                    scale=1.0,
+                    accum_out=sT[:, j, 8 * i + b : 8 * i + b + 1],
+                )
+
+        def perm_copy(dst_rows, tb, hh):
+            nc.scalar.copy(
+                out=dst_rows.rearrange("t (q j b) -> t q j b", q=4, j=8)[:, :, 4 * hh : 4 * hh + 4, :],
+                in_=tb[:].rearrange("t (j q b) -> t q j b", j=4, q=4),
+            )
+
+        def back_pe(i, sb):
+            xp = xts[i][1]
+            xs = xsp.tile([P, OUTC], F32, tag="xs", name="xs")
+            for hh in range(2):
+                tb = psum_tile([P, 512], "tr", "tb")
+                for jj in range(4):
+                    nc.tensor.transpose(
+                        tb[:, jj * P : (jj + 1) * P],
+                        xp[:, hh * 4 + jj, 2 * sb : 2 * sb + 2, :].rearrange("p b q -> p (b q)"),
+                        ident[:],
+                    )
+                perm_copy(xs[:], tb, hh)
+            row = (8 * i + 4 + 2 * sb) * 64
+            nc.sync.dma_start(out=xp_rows[row : row + P, :], in_=xs[:])
+
+        def back_ve(i):
+            xv = xts[i][0]
+            vt = r8.tile([P, 2048], F32, tag="r8", name="vt", align_bytes=64)
+            nc.vector.transpose(out=vt[:], in_=xv[:].rearrange("p s j a -> p (s j a)"))
+            row = 8 * i * 64
+            for q in range(4):
+                nc.sync.dma_start(
+                    out=xp_rows[row : row + 256, 256 * q : 256 * (q + 1)].rearrange("(s a) c -> a s c", a=32),
+                    in_=vt[32 * q : 32 * (q + 1), :].rearrange("p (s c) -> p s c", s=8),
+                )
 
         def sums_out(hf):
             so = xsp.tile([P, OUTC], F32, tag="xs", name="so")
@@ -252,34 +291,93 @@ def tile_pairwiserelationmodule_pa_l_kernel(tc, objs, W1, b1, W2, b2, out_0, out
                 tb = psum_tile([P, 512], "tr", "tbs")
                 for jj in range(4):
                     nc.tensor.transpose(
-                        tb[:, jj * P : (jj + 1) * P],
-                        sT[:, hh * 4 + jj, hf * P : (hf + 1) * P],
-                        ident[:],
+                        tb[:, jj * P : (jj + 1) * P], sT[:, hh * 4 + jj, hf * P : (hf + 1) * P], ident[:]
                     )
-                if hh == 0:
-                    nc.vector.tensor_copy(out=so[:, 0:512], in_=tb[:])
-                else:
-                    nc.scalar.copy(out=so[:, 512:1024], in_=tb[:])
+                perm_copy(so[:], tb, hh)
             nc.sync.dma_start(out=out_1[hf * P : (hf + 1) * P, :], in_=so[:])
 
-        prep_objs(0, True)
-        prep_weights(w1raw, 4, 1024, 4, w1c, w1s)
-        w2raw = big.tile([P, 8, HID], BF16, tag="big16", name="w2raw")
-        nc.sync.dma_start(out=w2raw[:], in_=W2.rearrange("(j m) g -> m j g", m=P))
-        stage1(0)
-        prep_weights([w2raw], 8, 512, 2, w2c, w2s)
-        hform(0)
-        for i in range(32):
-            if i % 2 == 1 and (i + 1) // 2 < 16:
-                stage1((i + 1) // 2)
-            if i + 1 < 32:
-                hform(i + 1)
-            stage2(i)
+        def oc_tiles(gq):
+            oc = ocp.tile([P, 4, 2, P], U32, tag="oc", name="oc", align_bytes=64)
+            osc = ocp.tile([P, 4, 2, P], U8, tag="osc", name="osc", align_bytes=64)
+            ocs[gq] = (oc, osc)
+
+        def quant_objs(gq, grp):
+            oc, osc = ocs[gq]
+            quant(grp, oc[:].rearrange("p s k c -> p (s k c)"), osc[:].rearrange("p s k c -> p (s k c)"))
+
+        load_bias()
+        oraw = {0: load_objs(0)}
+        w1raw = [load_w1(kk) for kk in range(4)]
+        w2raw = [load_w2(0)]
+        prep_bias()
+
+        grp = grp_tile()
+        for sp in range(4):
+            plain_bank(oraw[0], grp, sp, "v" if sp == 0 else "s", True)
+        oc_tiles(0)
+        quant_objs(0, grp)
+        w2raw.append(load_w2(1))
+        for kk in range(4):
+            grp = grp_tile()
+            for sp in range(4):
+                plain_bank(w1raw[kk], grp, sp, "v" if sp == 0 else "s", True)
+            quant(grp, w1c[:, kk, :], w1s[:, kk, :])
+            if kk == 0:
+                oraw[1] = load_objs(1)
+        stage1_half(0, 0)
+        stage1_half(0, 1)
+        h_add(0)
+        grp = grp_tile()
+        for sp in range(4):
+            w2_bank(w2raw[0], grp, sp, "s")
+        quant(grp, w2c[:, 0, :], w2s[:, 0, :])
+        h_relu(0)
+        grp = grp_tile()
+        for sp in range(4):
+            w2_bank(w2raw[1], grp, sp, "s")
+        quant(grp, w2c[:, 1, :], w2s[:, 1, :])
+        h_quant(0)
+        stage1_half(1, 0)
+        stage1_half(1, 1)
+        h_add(1)
+        h_relu(1)
+        h_quant(1)
+
+        ogrp = {}
+        for i in range(N_BLOCKS):
+            nxt = i + 2
+            if nxt < N_BLOCKS:
+                h_add(nxt)
+                h_relu(nxt)
+            stage2_open(i)
+            for j in range(4):
+                stage2(i, j)
             if i >= 1:
-                turn_back(i - 1)
-            if i == 1:
-                prep_objs(1, False)
+                back_ve(i - 1)
+                back_pe(i - 1, 0)
+            if nxt < N_BLOCKS:
+                h_quant(nxt)
+            for j in range(4, 8):
+                stage2(i, j)
+            if i % 2 == 0 and (i + 4) // 2 < N_UNITS:
+                stage1_half((i + 4) // 2, 0)
+            if i % 2 == 1 and (i + 3) // 2 < N_UNITS:
+                stage1_half((i + 3) // 2, 1)
+            if i >= 1:
+                back_pe(i - 1, 1)
+            gq, sp = divmod(i + 8, 8)
+            if gq < 4 and sp < 4:
+                if sp == 0:
+                    ogrp[gq] = grp_tile()
+                plain_bank(oraw[gq], ogrp[gq], sp, "v", False)
+                if sp == 3:
+                    oc_tiles(gq)
+                    quant_objs(gq, ogrp[gq])
+            if i == 4 or i == 12:
+                oraw[i // 8 + 2] = load_objs(i // 8 + 2)
             if i == 17:
                 sums_out(0)
-        turn_back(31)
+        back_ve(N_BLOCKS - 1)
+        back_pe(N_BLOCKS - 1, 0)
+        back_pe(N_BLOCKS - 1, 1)
         sums_out(1)

@@ -17,6 +17,8 @@ HID, OUTC = 1024, 1024
 FLOPS = 2 * (SETS * OBJ) * (2 * D) * HID + 2 * (SETS * OBJ * OBJ) * HID * OUTC
 N_BLOCKS = 32
 N_UNITS = 16
+GB = 6
+WIDE = 2
 
 
 def tile_pairwiserelationmodule_pa_l_kernel(tc, objs, W1, b1, W2, b2, out_0, out_1):
@@ -27,7 +29,8 @@ def tile_pairwiserelationmodule_pa_l_kernel(tc, objs, W1, b1, W2, b2, out_0, out
     with ExitStack() as ctx:
         const = ctx.enter_context(tc.tile_pool(name="const", bufs=1))
         r8 = ctx.enter_context(tc.tile_pool(name="r8", bufs=6))
-        mid = ctx.enter_context(tc.tile_pool(name="mid", bufs=3))
+        mid = ctx.enter_context(tc.tile_pool(name="mid", bufs=2))
+        hbp = ctx.enter_context(tc.tile_pool(name="hbp", bufs=2))
         xvp = ctx.enter_context(tc.tile_pool(name="xvp", bufs=2))
         ocp = ctx.enter_context(tc.tile_pool(name="ocp", bufs=2))
         abp = ctx.enter_context(tc.tile_pool(name="abp", bufs=2))
@@ -63,7 +66,7 @@ def tile_pairwiserelationmodule_pa_l_kernel(tc, objs, W1, b1, W2, b2, out_0, out
         w1s = const.tile([P, 4, HID], U8, name="w1s", align_bytes=64)
         w2c = const.tile([P, 2, OUTC], U32, name="w2c", align_bytes=64)
         w2s = const.tile([P, 2, OUTC], U8, name="w2s", align_bytes=64)
-        sT = const.tile([P, 8, SETS], F32, name="sT")
+        sT = const.tile([P, 8, 8, N_BLOCKS], F32, name="sT")
         b1t = const.tile([P, 2, 4], F32, name="b1t")
         b2t = const.tile([P, 8], F32, name="b2t")
         zall = const.tile([P, 640], BF16, name="zall")
@@ -159,9 +162,9 @@ def tile_pairwiserelationmodule_pa_l_kernel(tc, objs, W1, b1, W2, b2, out_0, out
         hq = {}
         xts = {}
 
-        def stage1_half(u, part):
+        def stage1_mm(u, part):
             oc, osc = ocs[u // 4]
-            dst = abp.tile([P, 2, P, 4], F32, tag="at" if part == 0 else "bt", name="abt")
+            banks = []
             for g in range(2):
                 ps = psum_tile([P, 4, P], "s1", "ps1")
                 for t in range(4):
@@ -176,7 +179,14 @@ def tile_pairwiserelationmodule_pa_l_kernel(tc, objs, W1, b1, W2, b2, out_0, out
                             start=(kk == 0),
                             stop=(kk == 1),
                         )
-                src = ps[:].rearrange("p t c -> p c t")
+                banks.append(ps)
+            return (u, part, banks)
+
+        def stage1_out(job, engine):
+            u, part, banks = job
+            dst = abp.tile([P, 2, P, 4], F32, tag="at" if part == 0 else "bt", name="abt")
+            for g in range(2):
+                src = banks[g][:].rearrange("p t c -> p c t")
                 if part == 0:
                     nc.vector.tensor_tensor(
                         out=dst[:, g],
@@ -184,37 +194,47 @@ def tile_pairwiserelationmodule_pa_l_kernel(tc, objs, W1, b1, W2, b2, out_0, out
                         in1=b1t[:, g, :].unsqueeze(1).to_broadcast([P, P, 4]),
                         op=ALU.add,
                     )
+                elif engine == "v":
+                    nc.vector.tensor_copy(out=dst[:, g], in_=src)
                 else:
                     nc.scalar.copy(out=dst[:, g], in_=src)
             ab[(u, part)] = dst
 
-        def h_add(i):
-            u, beta = divmod(i, 2)
-            at = ab[(u, 0)]
-            bt = ab[(u, 1)]
-            hb = mid.tile([P, 2, 512, 4], BF16, tag="mid8", name="hb", align_bytes=64)
-            cols = slice(beta * 64, (beta + 1) * 64)
-            for g in range(2):
-                nc.vector.tensor_tensor(
-                    out=hb[:, g].rearrange("p (b k m) t -> p b k m t", b=8, k=8),
-                    in0=at[:, g, cols, :].rearrange("p (b m) t -> p b m t", b=8).unsqueeze(2).to_broadcast([P, 8, 8, 8, 4]),
-                    in1=bt[:, g, cols, :].rearrange("p (b k) t -> p b k t", b=8).unsqueeze(3).to_broadcast([P, 8, 8, 8, 4]),
-                    op=ALU.add,
-                )
-            hbs[i] = hb
+        def h_piece(engine, n, hb, g, b0, b1):
+            u, beta = divmod(n, 2)
+            nb = b1 - b0
+            cols = slice(beta * 64 + 8 * b0, beta * 64 + 8 * b1)
+            engine.tensor_tensor(
+                out=hb[:, 64 * b0 : 64 * b1, :].rearrange("p (b k m) t -> p b k m t", b=nb, k=8),
+                in0=ab[(u, 0)][:, g, cols, :].rearrange("p (b m) t -> p b m t", b=nb).unsqueeze(2).to_broadcast([P, nb, 8, 8, 4]),
+                in1=ab[(u, 1)][:, g, cols, :].rearrange("p (b k) t -> p b k t", b=nb).unsqueeze(3).to_broadcast([P, nb, 8, 8, 4]),
+                op=ALU.add,
+            )
 
-        def h_relu(i):
-            for g in range(2):
-                flat = hbs[i][:, g].rearrange("p c t -> p (c t)")
+        def h_add(n, gb):
+            hb0 = hbp.tile([P, 512, 4], BF16, tag="hb0", name="hb0", align_bytes=64)
+            hb1 = hbp.tile([P, 512, 4], BF16, tag="hb1", name="hb1", align_bytes=64, bufs=1)
+            if gb > 0:
+                h_piece(nc.gpsimd, n, hb1, 1, 8 - gb, 8)
+            h_piece(nc.vector, n, hb0, 0, 0, 8)
+            if gb < 8:
+                h_piece(nc.vector, n, hb1, 1, 0, 8 - gb)
+            hbs[n] = (hb0, hb1)
+
+        def h_relu(n):
+            for hb in hbs[n]:
+                flat = hb[:].rearrange("p c t -> p (c t)")
                 nc.vector.tensor_scalar_max(out=flat, in0=flat, scalar1=0.0)
 
-        def h_quant(i):
+        def h_quant(n):
             hc = cod.tile([P, 1024], U32, tag="hc", name="hc", align_bytes=64)
             hs = cod.tile([P, 1024], U8, tag="hs", name="hs", align_bytes=64)
-            nc.vector.quantize_mx(
-                out=hc[:].bitcast(FP8X4), scales=hs[:], in_=hbs[i][:].rearrange("p g c t -> p (g c t)")
-            )
-            hq[i] = (hc, hs)
+            for g in range(2):
+                tok = slice(g * 512, (g + 1) * 512)
+                nc.vector.quantize_mx(
+                    out=hc[:, tok].bitcast(FP8X4), scales=hs[:, tok], in_=hbs[n][g][:].rearrange("p c t -> p (c t)")
+                )
+            hq[n] = (hc, hs)
 
         def stage2_open(i):
             xv = xvp.tile([P, 8, 8, 32], F32, tag="xv", name="xv", align_bytes=64, bufs=3)
@@ -237,7 +257,14 @@ def tile_pairwiserelationmodule_pa_l_kernel(tc, objs, W1, b1, W2, b2, out_0, out
                     start=(g == 0),
                     stop=(g == 1),
                 )
-            for b in range(8):
+            nc.scalar.activation(
+                out=xv[:, 0 : 2 * WIDE, j, :],
+                in_=y[:, 0 : 64 * WIDE].rearrange("p (s a) -> p s a", a=32),
+                func=ACT.Relu,
+                bias=b2t[:, j : j + 1],
+                scale=1.0,
+            )
+            for b in range(WIDE, 8):
                 src = y[:, 64 * b : 64 * (b + 1)]
                 if b < 4:
                     dst = xv[:, 2 * b : 2 * b + 2, j, :]
@@ -250,13 +277,24 @@ def tile_pairwiserelationmodule_pa_l_kernel(tc, objs, W1, b1, W2, b2, out_0, out
                     func=ACT.Relu,
                     bias=b2t[:, j : j + 1],
                     scale=1.0,
-                    accum_out=sT[:, j, 8 * i + b : 8 * i + b + 1],
+                    accum_out=sT[:, j, b, i : i + 1],
                 )
 
-        def perm_copy(dst_rows, tb, hh):
-            nc.scalar.copy(
-                out=dst_rows.rearrange("t (q j b) -> t q j b", q=4, j=8)[:, :, 4 * hh : 4 * hh + 4, :],
-                in_=tb[:].rearrange("t (j q b) -> t q j b", j=4, q=4),
+        def wide_sums(i):
+            xv = xts[i][0]
+            for b in range(WIDE):
+                nc.vector.tensor_reduce(
+                    out=sT[:, :, b, i],
+                    in_=xv[:, 2 * b : 2 * b + 2, :, :].rearrange("p s j a -> p j s a"),
+                    axis=mybir.AxisListType.XY,
+                    op=ALU.add,
+                )
+
+        def perm_copy(engine, dst_rows, tb, hh):
+            word_copy(
+                engine,
+                dst_rows.rearrange("t (q j b) -> t q j b", q=4, j=8)[:, :, 4 * hh : 4 * hh + 4, :],
+                tb[:].rearrange("t (j q b) -> t q j b", j=4, q=4),
             )
 
         def back_pe(i, sb):
@@ -270,7 +308,7 @@ def tile_pairwiserelationmodule_pa_l_kernel(tc, objs, W1, b1, W2, b2, out_0, out
                         xp[:, hh * 4 + jj, 2 * sb : 2 * sb + 2, :].rearrange("p b q -> p (b q)"),
                         ident[:],
                     )
-                perm_copy(xs[:], tb, hh)
+                perm_copy("s", xs[:], tb, hh)
             row = (8 * i + 4 + 2 * sb) * 64
             nc.sync.dma_start(out=xp_rows[row : row + P, :], in_=xs[:])
 
@@ -285,16 +323,20 @@ def tile_pairwiserelationmodule_pa_l_kernel(tc, objs, W1, b1, W2, b2, out_0, out
                     in_=vt[32 * q : 32 * (q + 1), :].rearrange("p (s c) -> p s c", s=8),
                 )
 
-        def sums_out(hf):
+        def sums_out(bq):
             so = xsp.tile([P, OUTC], F32, tag="xs", name="so")
             for hh in range(2):
                 tb = psum_tile([P, 512], "tr", "tbs")
                 for jj in range(4):
                     nc.tensor.transpose(
-                        tb[:, jj * P : (jj + 1) * P], sT[:, hh * 4 + jj, hf * P : (hf + 1) * P], ident[:]
+                        tb[:, jj * P : (jj + 1) * P],
+                        sT[:, hh * 4 + jj, 4 * bq : 4 * bq + 4, :].rearrange("p b i -> p (b i)"),
+                        ident[:],
                     )
-                perm_copy(so[:], tb, hh)
-            nc.sync.dma_start(out=out_1[hf * P : (hf + 1) * P, :], in_=so[:])
+                perm_copy("s" if hh == 0 else "v", so[:], tb, hh)
+            by_b = out_1.rearrange("(i b) c -> b i c", b=8)
+            for bl in range(4):
+                nc.sync.dma_start(out=by_b[4 * bq + bl], in_=so[32 * bl : 32 * (bl + 1), :])
 
         def oc_tiles(gq):
             oc = ocp.tile([P, 4, 2, P], U32, tag="oc", name="oc", align_bytes=64)
@@ -302,8 +344,21 @@ def tile_pairwiserelationmodule_pa_l_kernel(tc, objs, W1, b1, W2, b2, out_0, out
             ocs[gq] = (oc, osc)
 
         def quant_objs(gq, grp):
+            oc_tiles(gq)
             oc, osc = ocs[gq]
             quant(grp, oc[:].rearrange("p s k c -> p (s k c)"), osc[:].rearrange("p s k c -> p (s k c)"))
+
+        def w1_chunk(kk):
+            grp = grp_tile()
+            for sp in range(4):
+                plain_bank(w1raw[kk], grp, sp, "v" if sp == 0 else "s", True)
+            quant(grp, w1c[:, kk, :], w1s[:, kk, :])
+
+        def w2_chunk(kk):
+            grp = grp_tile()
+            for sp in range(4):
+                w2_bank(w2raw[kk], grp, sp, "s")
+            quant(grp, w2c[:, kk, :], w2s[:, kk, :])
 
         load_bias()
         oraw = {0: load_objs(0)}
@@ -314,70 +369,73 @@ def tile_pairwiserelationmodule_pa_l_kernel(tc, objs, W1, b1, W2, b2, out_0, out
         grp = grp_tile()
         for sp in range(4):
             plain_bank(oraw[0], grp, sp, "v" if sp == 0 else "s", True)
-        oc_tiles(0)
         quant_objs(0, grp)
         w2raw.append(load_w2(1))
-        for kk in range(4):
-            grp = grp_tile()
-            for sp in range(4):
-                plain_bank(w1raw[kk], grp, sp, "v" if sp == 0 else "s", True)
-            quant(grp, w1c[:, kk, :], w1s[:, kk, :])
-            if kk == 0:
-                oraw[1] = load_objs(1)
-        stage1_half(0, 0)
-        stage1_half(0, 1)
-        h_add(0)
-        grp = grp_tile()
-        for sp in range(4):
-            w2_bank(w2raw[0], grp, sp, "s")
-        quant(grp, w2c[:, 0, :], w2s[:, 0, :])
+        w1_chunk(0)
+        oraw[1] = load_objs(1)
+        w1_chunk(1)
+        for u in range(2):
+            stage1_out(stage1_mm(u, 0), "v")
+        w1_chunk(2)
+        w1_chunk(3)
+        for u in range(2):
+            stage1_out(stage1_mm(u, 1), "s")
+        h_add(0, 0)
+        w2_chunk(0)
         h_relu(0)
-        grp = grp_tile()
-        for sp in range(4):
-            w2_bank(w2raw[1], grp, sp, "s")
-        quant(grp, w2c[:, 1, :], w2s[:, 1, :])
+        w2_chunk(1)
         h_quant(0)
-        stage1_half(1, 0)
-        stage1_half(1, 1)
-        h_add(1)
+        h_add(1, 0)
         h_relu(1)
         h_quant(1)
 
+        OBJ_STEPS = {0: [(1, 0), (1, 1)], 1: [(1, 2)], 2: [(1, 3)]}
+        for gq in (2, 3):
+            for sp in range(4):
+                OBJ_STEPS[8 * gq - 10 + sp] = [(gq, sp)]
         ogrp = {}
+        jobs = [stage1_mm(2, 0)]
+        quants = []
         for i in range(N_BLOCKS):
-            nxt = i + 2
-            if nxt < N_BLOCKS:
-                h_add(nxt)
-                h_relu(nxt)
+            n = i + 2
+            for job in jobs:
+                stage1_out(job, "v")
+            jobs = []
+            if i >= 1:
+                wide_sums(i - 1)
+                back_ve(i - 1)
+            for gq in quants:
+                quant_objs(gq, ogrp[gq])
+            quants = []
+            if n < N_BLOCKS:
+                h_add(n, GB)
+                h_relu(n)
+                h_quant(n)
             stage2_open(i)
             for j in range(4):
                 stage2(i, j)
             if i >= 1:
-                back_ve(i - 1)
                 back_pe(i - 1, 0)
-            if nxt < N_BLOCKS:
-                h_quant(nxt)
             for j in range(4, 8):
                 stage2(i, j)
+            if i % 2 == 1 and (i + 5) // 2 < N_UNITS:
+                jobs.append(stage1_mm((i + 5) // 2, 0))
             if i % 2 == 0 and (i + 4) // 2 < N_UNITS:
-                stage1_half((i + 4) // 2, 0)
-            if i % 2 == 1 and (i + 3) // 2 < N_UNITS:
-                stage1_half((i + 3) // 2, 1)
+                jobs.append(stage1_mm((i + 4) // 2, 1))
             if i >= 1:
                 back_pe(i - 1, 1)
-            gq, sp = divmod(i + 8, 8)
-            if gq < 4 and sp < 4:
+            for gq, sp in OBJ_STEPS.get(i, []):
                 if sp == 0:
                     ogrp[gq] = grp_tile()
-                plain_bank(oraw[gq], ogrp[gq], sp, "v", False)
+                plain_bank(oraw[gq], ogrp[gq], sp, "s", False)
                 if sp == 3:
-                    oc_tiles(gq)
-                    quant_objs(gq, ogrp[gq])
-            if i == 4 or i == 12:
+                    quants.append(gq)
+            if i == 2 or i == 10:
                 oraw[i // 8 + 2] = load_objs(i // 8 + 2)
-            if i == 17:
-                sums_out(0)
-        back_ve(N_BLOCKS - 1)
-        back_pe(N_BLOCKS - 1, 0)
-        back_pe(N_BLOCKS - 1, 1)
+        last = N_BLOCKS - 1
+        wide_sums(last)
+        back_ve(last)
+        back_pe(last, 0)
+        back_pe(last, 1)
+        sums_out(0)
         sums_out(1)

@@ -17,7 +17,7 @@ HID, OUTC = 1024, 1024
 FLOPS = 2 * (SETS * OBJ) * (2 * D) * HID + 2 * (SETS * OBJ * OBJ) * HID * OUTC
 N_BLOCKS = 32
 N_UNITS = 16
-GB = 6
+G_SETS0 = 1
 WIDE = 2
 
 
@@ -62,8 +62,8 @@ def tile_pairwiserelationmodule_pa_l_kernel(tc, objs, W1, b1, W2, b2, out_0, out
         ident = const.tile([P, P], F32, name="ident")
         make_identity(nc, ident[:])
 
-        w1c = const.tile([P, 4, HID], U32, name="w1c", align_bytes=64)
-        w1s = const.tile([P, 4, HID], U8, name="w1s", align_bytes=64)
+        w1c = const.tile([P, 2, 2, 4, 2, P], U32, name="w1c", align_bytes=64)
+        w1s = const.tile([P, 2, 2, 4, 2, P], U8, name="w1s", align_bytes=64)
         w2c = const.tile([P, 2, OUTC], U32, name="w2c", align_bytes=64)
         w2s = const.tile([P, 2, OUTC], U8, name="w2s", align_bytes=64)
         sT = const.tile([P, 8, 8, N_BLOCKS], F32, name="sT")
@@ -91,13 +91,12 @@ def tile_pairwiserelationmodule_pa_l_kernel(tc, objs, W1, b1, W2, b2, out_0, out
             )
             return raw
 
-        def load_w1(kk):
+        def load_w1(g, part):
             raw = raw_tile()
-            for g in range(2):
-                nc.sync.dma_start(
-                    out=raw[:, 4 * g : 4 * g + 4, :],
-                    in_=W1[512 * g : 512 * (g + 1), 512 * kk : 512 * (kk + 1)].rearrange("(m t) k -> m t k", t=4),
-                )
+            nc.sync.dma_start(
+                out=raw[:].rearrange("p (t k) d -> p t (k d)", k=2),
+                in_=W1[512 * g : 512 * (g + 1), 1024 * part : 1024 * (part + 1)].rearrange("(m t) k -> m t k", t=4),
+            )
             return raw
 
         def load_w2(kk):
@@ -162,31 +161,32 @@ def tile_pairwiserelationmodule_pa_l_kernel(tc, objs, W1, b1, W2, b2, out_0, out
         hq = {}
         xts = {}
 
-        def stage1_mm(u, part):
+        def stage1_mm(u, pairs):
             oc, osc = ocs[u // 4]
             banks = []
-            for g in range(2):
+            for part, g in pairs:
                 ps = psum_tile([P, 4, P], "s1", "ps1")
                 for t in range(4):
-                    wcol = slice((g * 4 + t) * P, (g * 4 + t + 1) * P)
                     for kk in range(2):
                         nc.tensor.matmul_mx(
                             out=ps[:, t, :],
-                            lhsT=w1c[:, 2 * part + kk, wcol].bitcast(FP8X4),
-                            lhsT_scale=w1s[:, 2 * part + kk, wcol],
+                            lhsT=w1c[:, g, part, t, kk, :].bitcast(FP8X4),
+                            lhsT_scale=w1s[:, g, part, t, kk, :],
                             rhs=oc[:, u % 4, kk, :].bitcast(FP8X4),
                             rhs_scale=osc[:, u % 4, kk, :],
                             start=(kk == 0),
                             stop=(kk == 1),
                         )
-                banks.append(ps)
-            return (u, part, banks)
+                banks.append((part, g, ps))
+            return (u, banks)
 
         def stage1_out(job, engine):
-            u, part, banks = job
-            dst = abp.tile([P, 2, P, 4], F32, tag="at" if part == 0 else "bt", name="abt")
-            for g in range(2):
-                src = banks[g][:].rearrange("p t c -> p c t")
+            u, banks = job
+            for part, g, ps in banks:
+                if (u, part) not in ab:
+                    ab[(u, part)] = abp.tile([P, 2, P, 4], F32, tag="at" if part == 0 else "bt", name="abt")
+                dst = ab[(u, part)]
+                src = ps[:].rearrange("p t c -> p c t")
                 if part == 0:
                     nc.vector.tensor_tensor(
                         out=dst[:, g],
@@ -198,7 +198,6 @@ def tile_pairwiserelationmodule_pa_l_kernel(tc, objs, W1, b1, W2, b2, out_0, out
                     nc.vector.tensor_copy(out=dst[:, g], in_=src)
                 else:
                     nc.scalar.copy(out=dst[:, g], in_=src)
-            ab[(u, part)] = dst
 
         def h_piece(engine, n, hb, g, b0, b1):
             u, beta = divmod(n, 2)
@@ -211,30 +210,34 @@ def tile_pairwiserelationmodule_pa_l_kernel(tc, objs, W1, b1, W2, b2, out_0, out
                 op=ALU.add,
             )
 
-        def h_add(n, gb):
+        def h_open(n):
             hb0 = hbp.tile([P, 512, 4], BF16, tag="hb0", name="hb0", align_bytes=64)
             hb1 = hbp.tile([P, 512, 4], BF16, tag="hb1", name="hb1", align_bytes=64, bufs=1)
-            if gb > 0:
-                h_piece(nc.gpsimd, n, hb1, 1, 8 - gb, 8)
-            h_piece(nc.vector, n, hb0, 0, 0, 8)
-            if gb < 8:
-                h_piece(nc.vector, n, hb1, 1, 0, 8 - gb)
-            hbs[n] = (hb0, hb1)
-
-        def h_relu(n):
-            for hb in hbs[n]:
-                flat = hb[:].rearrange("p c t -> p (c t)")
-                nc.vector.tensor_scalar_max(out=flat, in0=flat, scalar1=0.0)
-
-        def h_quant(n):
             hc = cod.tile([P, 1024], U32, tag="hc", name="hc", align_bytes=64)
             hs = cod.tile([P, 1024], U8, tag="hs", name="hs", align_bytes=64)
-            for g in range(2):
-                tok = slice(g * 512, (g + 1) * 512)
-                nc.vector.quantize_mx(
-                    out=hc[:, tok].bitcast(FP8X4), scales=hs[:, tok], in_=hbs[n][g][:].rearrange("p c t -> p (c t)")
-                )
+            hbs[n] = (hb0, hb1)
             hq[n] = (hc, hs)
+
+        def h_relu(n, g):
+            flat = hbs[n][g][:].rearrange("p c t -> p (c t)")
+            nc.vector.tensor_scalar_max(out=flat, in0=flat, scalar1=0.0)
+
+        def h_quant(n, g):
+            hc, hs = hq[n]
+            tok = slice(g * 512, (g + 1) * 512)
+            nc.vector.quantize_mx(
+                out=hc[:, tok].bitcast(FP8X4), scales=hs[:, tok], in_=hbs[n][g][:].rearrange("p c t -> p (c t)")
+            )
+
+        def h_all(n):
+            h_open(n)
+            h_piece(nc.gpsimd, n, hbs[n][1], 1, 0, 8)
+            h_piece(nc.gpsimd, n, hbs[n][0], 0, 8 - G_SETS0, 8)
+            h_piece(nc.vector, n, hbs[n][0], 0, 0, 8 - G_SETS0)
+            h_relu(n, 1)
+            h_relu(n, 0)
+            h_quant(n, 1)
+            h_quant(n, 0)
 
         def stage2_open(i):
             xv = xvp.tile([P, 8, 8, 32], F32, tag="xv", name="xv", align_bytes=64, bufs=3)
@@ -297,7 +300,7 @@ def tile_pairwiserelationmodule_pa_l_kernel(tc, objs, W1, b1, W2, b2, out_0, out
                 tb[:].rearrange("t (j q b) -> t q j b", j=4, q=4),
             )
 
-        def back_pe(i, sb):
+        def back_pe(i, sb, engine):
             xp = xts[i][1]
             xs = xsp.tile([P, OUTC], F32, tag="xs", name="xs")
             for hh in range(2):
@@ -308,7 +311,7 @@ def tile_pairwiserelationmodule_pa_l_kernel(tc, objs, W1, b1, W2, b2, out_0, out
                         xp[:, hh * 4 + jj, 2 * sb : 2 * sb + 2, :].rearrange("p b q -> p (b q)"),
                         ident[:],
                     )
-                perm_copy("s", xs[:], tb, hh)
+                perm_copy(engine, xs[:], tb, hh)
             row = (8 * i + 4 + 2 * sb) * 64
             nc.sync.dma_start(out=xp_rows[row : row + P, :], in_=xs[:])
 
@@ -348,11 +351,15 @@ def tile_pairwiserelationmodule_pa_l_kernel(tc, objs, W1, b1, W2, b2, out_0, out
             oc, osc = ocs[gq]
             quant(grp, oc[:].rearrange("p s k c -> p (s k c)"), osc[:].rearrange("p s k c -> p (s k c)"))
 
-        def w1_chunk(kk):
+        def w1_chunk(g, part):
             grp = grp_tile()
             for sp in range(4):
-                plain_bank(w1raw[kk], grp, sp, "v" if sp == 0 else "s", True)
-            quant(grp, w1c[:, kk, :], w1s[:, kk, :])
+                plain_bank(w1raw[(g, part)], grp, sp, "v" if (sp == 0 and g == 0) else "s", True)
+            quant(
+                grp,
+                w1c[:, g, part].rearrange("p t k m -> p (t k m)"),
+                w1s[:, g, part].rearrange("p t k m -> p (t k m)"),
+            )
 
         def w2_chunk(kk):
             grp = grp_tile()
@@ -362,7 +369,10 @@ def tile_pairwiserelationmodule_pa_l_kernel(tc, objs, W1, b1, W2, b2, out_0, out
 
         load_bias()
         oraw = {0: load_objs(0)}
-        w1raw = [load_w1(kk) for kk in range(4)]
+        w1raw = {}
+        for g in range(2):
+            for part in range(2):
+                w1raw[(g, part)] = load_w1(g, part)
         w2raw = [load_w2(0)]
         prep_bias()
 
@@ -371,30 +381,38 @@ def tile_pairwiserelationmodule_pa_l_kernel(tc, objs, W1, b1, W2, b2, out_0, out
             plain_bank(oraw[0], grp, sp, "v" if sp == 0 else "s", True)
         quant_objs(0, grp)
         w2raw.append(load_w2(1))
-        w1_chunk(0)
+        w1_chunk(0, 0)
         oraw[1] = load_objs(1)
-        w1_chunk(1)
-        for u in range(2):
-            stage1_out(stage1_mm(u, 0), "v")
-        w1_chunk(2)
-        w1_chunk(3)
-        for u in range(2):
-            stage1_out(stage1_mm(u, 1), "s")
-        h_add(0, 0)
+        w1_chunk(0, 1)
+        h_open(0)
+        stage1_out(stage1_mm(0, [(0, 0), (1, 0)]), "s")
+        h_piece(nc.vector, 0, hbs[0][0], 0, 0, 8)
+        w1_chunk(1, 0)
+        h_relu(0, 0)
+        w1_chunk(1, 1)
+        h_quant(0, 0)
+        stage1_out(stage1_mm(0, [(0, 1), (1, 1)]), "s")
+        h_piece(nc.vector, 0, hbs[0][1], 1, 0, 8)
         w2_chunk(0)
-        h_relu(0)
+        h_relu(0, 1)
         w2_chunk(1)
-        h_quant(0)
-        h_add(1, 0)
-        h_relu(1)
-        h_quant(1)
+        h_quant(0, 1)
+        stage1_out(stage1_mm(1, [(0, 0), (1, 0)]), "s")
+        stage1_out(stage1_mm(1, [(0, 1), (1, 1)]), "s")
+        h_open(1)
+        h_piece(nc.vector, 1, hbs[1][0], 0, 0, 8)
+        h_piece(nc.vector, 1, hbs[1][1], 1, 0, 8)
+        h_relu(1, 0)
+        h_relu(1, 1)
+        h_quant(1, 0)
+        h_quant(1, 1)
 
         OBJ_STEPS = {0: [(1, 0), (1, 1)], 1: [(1, 2)], 2: [(1, 3)]}
         for gq in (2, 3):
             for sp in range(4):
                 OBJ_STEPS[8 * gq - 10 + sp] = [(gq, sp)]
         ogrp = {}
-        jobs = [stage1_mm(2, 0)]
+        jobs = [stage1_mm(2, [(0, 0), (0, 1)])]
         quants = []
         for i in range(N_BLOCKS):
             n = i + 2
@@ -408,22 +426,21 @@ def tile_pairwiserelationmodule_pa_l_kernel(tc, objs, W1, b1, W2, b2, out_0, out
                 quant_objs(gq, ogrp[gq])
             quants = []
             if n < N_BLOCKS:
-                h_add(n, GB)
-                h_relu(n)
-                h_quant(n)
+                h_all(n)
             stage2_open(i)
             for j in range(4):
                 stage2(i, j)
+            late = "v" if n >= N_BLOCKS else "s"
             if i >= 1:
-                back_pe(i - 1, 0)
+                back_pe(i - 1, 0, late)
             for j in range(4, 8):
                 stage2(i, j)
             if i % 2 == 1 and (i + 5) // 2 < N_UNITS:
-                jobs.append(stage1_mm((i + 5) // 2, 0))
+                jobs.append(stage1_mm((i + 5) // 2, [(0, 0), (0, 1)]))
             if i % 2 == 0 and (i + 4) // 2 < N_UNITS:
-                jobs.append(stage1_mm((i + 4) // 2, 1))
+                jobs.append(stage1_mm((i + 4) // 2, [(1, 0), (1, 1)]))
             if i >= 1:
-                back_pe(i - 1, 1)
+                back_pe(i - 1, 1, late)
             for gq, sp in OBJ_STEPS.get(i, []):
                 if sp == 0:
                     ogrp[gq] = grp_tile()
@@ -435,7 +452,7 @@ def tile_pairwiserelationmodule_pa_l_kernel(tc, objs, W1, b1, W2, b2, out_0, out
         last = N_BLOCKS - 1
         wide_sums(last)
         back_ve(last)
-        back_pe(last, 0)
-        back_pe(last, 1)
+        back_pe(last, 0, "s")
+        back_pe(last, 1, "s")
         sums_out(0)
         sums_out(1)

@@ -17,7 +17,7 @@ HID, OUTC = 1024, 1024
 FLOPS = 2 * (SETS * OBJ) * (2 * D) * HID + 2 * (SETS * OBJ * OBJ) * HID * OUTC
 N_BLOCKS = 32
 N_UNITS = 16
-G_SETS0 = 1
+G_SETS0 = 2
 WIDE = 2
 
 
@@ -300,9 +300,9 @@ def tile_pairwiserelationmodule_pa_l_kernel(tc, objs, W1, b1, W2, b2, out_0, out
                 tb[:].rearrange("t (j q b) -> t q j b", j=4, q=4),
             )
 
-        def back_pe(i, sb, engine):
+        def back_pe_turn(i, sb):
             xp = xts[i][1]
-            xs = xsp.tile([P, OUTC], F32, tag="xs", name="xs")
+            banks = []
             for hh in range(2):
                 tb = psum_tile([P, 512], "tr", "tb")
                 for jj in range(4):
@@ -311,7 +311,14 @@ def tile_pairwiserelationmodule_pa_l_kernel(tc, objs, W1, b1, W2, b2, out_0, out
                         xp[:, hh * 4 + jj, 2 * sb : 2 * sb + 2, :].rearrange("p b q -> p (b q)"),
                         ident[:],
                     )
-                perm_copy(engine, xs[:], tb, hh)
+                banks.append(tb)
+            return (i, sb, banks)
+
+        def back_pe_out(turned, engine):
+            i, sb, banks = turned
+            xs = xsp.tile([P, OUTC], F32, tag="xs", name="xs")
+            for hh in range(2):
+                perm_copy(engine, xs[:], banks[hh], hh)
             row = (8 * i + 4 + 2 * sb) * 64
             nc.sync.dma_start(out=xp_rows[row : row + P, :], in_=xs[:])
 
@@ -414,11 +421,15 @@ def tile_pairwiserelationmodule_pa_l_kernel(tc, objs, W1, b1, W2, b2, out_0, out
         ogrp = {}
         jobs = [stage1_mm(2, [(0, 0), (0, 1)])]
         quants = []
+        waiting = []
         for i in range(N_BLOCKS):
             n = i + 2
             for job in jobs:
                 stage1_out(job, "v")
             jobs = []
+            for turned in waiting:
+                back_pe_out(turned, "v")
+            waiting = []
             if i >= 1:
                 wide_sums(i - 1)
                 back_ve(i - 1)
@@ -432,7 +443,7 @@ def tile_pairwiserelationmodule_pa_l_kernel(tc, objs, W1, b1, W2, b2, out_0, out
                 stage2(i, j)
             late = "v" if n >= N_BLOCKS else "s"
             if i >= 1:
-                back_pe(i - 1, 0, late)
+                back_pe_out(back_pe_turn(i - 1, 0), late)
             for j in range(4, 8):
                 stage2(i, j)
             if i % 2 == 1 and (i + 5) // 2 < N_UNITS:
@@ -440,7 +451,7 @@ def tile_pairwiserelationmodule_pa_l_kernel(tc, objs, W1, b1, W2, b2, out_0, out
             if i % 2 == 0 and (i + 4) // 2 < N_UNITS:
                 jobs.append(stage1_mm((i + 4) // 2, [(1, 0), (1, 1)]))
             if i >= 1:
-                back_pe(i - 1, 1, late)
+                waiting.append(back_pe_turn(i - 1, 1))
             for gq, sp in OBJ_STEPS.get(i, []):
                 if sp == 0:
                     ogrp[gq] = grp_tile()
@@ -450,9 +461,11 @@ def tile_pairwiserelationmodule_pa_l_kernel(tc, objs, W1, b1, W2, b2, out_0, out
             if i == 2 or i == 10:
                 oraw[i // 8 + 2] = load_objs(i // 8 + 2)
         last = N_BLOCKS - 1
+        for turned in waiting:
+            back_pe_out(turned, "v")
         wide_sums(last)
         back_ve(last)
-        back_pe(last, 0, "s")
-        back_pe(last, 1, "s")
+        back_pe_out(back_pe_turn(last, 0), "s")
+        back_pe_out(back_pe_turn(last, 1), "s")
         sums_out(0)
         sums_out(1)

from contextlib import ExitStack

import concourse.mybir as mybir
from concourse.masks import make_identity

F32 = mybir.dt.float32
BF16 = mybir.dt.bfloat16
U32 = mybir.dt.uint32
U8 = mybir.dt.uint8
FP8X4 = mybir.dt.float8_e4m3fn_x4
ACT = mybir.ActivationFunctionType
ALU = mybir.AluOpType

P = 128
SETS, OBJ, D = 256, 8, 1024
HID, OUTC = 1024, 1024
FLOPS = 2 * (SETS * OBJ) * (2 * D) * HID + 2 * (SETS * OBJ * OBJ) * HID * OUTC
N_BLOCKS = 32
N_UNITS = 16
G_SETS0 = 2
WIDE = 2


def tile_pairwiserelationmodule_pa_l_kernel(tc, objs, W1, b1, W2, b2, out_0, out_1):
    nc = tc.nc
    xp_rows = out_0.flatten_outer_dims()
    obj_rows = objs.flatten_outer_dims()

    with ExitStack() as ctx:
        const = ctx.enter_context(tc.tile_pool(name="const", bufs=1))
        r8 = ctx.enter_context(tc.tile_pool(name="r8", bufs=6))
        mid = ctx.enter_context(tc.tile_pool(name="mid", bufs=2))
        hbp = ctx.enter_context(tc.tile_pool(name="hbp", bufs=2))
        xvp = ctx.enter_context(tc.tile_pool(name="xvp", bufs=2))
        ocp = ctx.enter_context(tc.tile_pool(name="ocp", bufs=2))
        abp = ctx.enter_context(tc.tile_pool(name="abp", bufs=2))
        cod = ctx.enter_context(tc.tile_pool(name="cod", bufs=4))
        xsp = ctx.enter_context(tc.tile_pool(name="xsp", bufs=4))
        psum = ctx.enter_context(tc.psum_pool(name="psum", bufs=2))
        ctx.enter_context(tc.manual_schedule())

        PS_BUFS = {"y": 4, "tr": 2, "s1": 2}
        HEAD_TAGS = ["y", "y", "tr", "y", "y", "tr"]
        state = {"head": 0}

        def psum_tile(shape, tag, name):
            return psum.tile(shape, F32, tag=tag, bufs=PS_BUFS[tag], name=name)

        def head_psum(in_head):
            tag = "tr"
            if in_head:
                tag = HEAD_TAGS[state["head"] % 6]
                state["head"] = state["head"] + 1
            return psum_tile([P, 2, 2, P], tag, "pt")

        def word_copy(engine, out, in_):
            if engine == "v":
                nc.vector.tensor_copy(out=out, in_=in_)
            else:
                nc.scalar.copy(out=out, in_=in_)

        ident = const.tile([P, P], F32, name="ident")
        make_identity(nc, ident[:])

        w1c = const.tile([P, 2, 2, 4, 2, P], U32, name="w1c", align_bytes=64)
        w1s = const.tile([P, 2, 2, 4, 2, P], U8, name="w1s", align_bytes=64)
        w2c = const.tile([P, 2, OUTC], U32, name="w2c", align_bytes=64)
        w2s = const.tile([P, 2, OUTC], U8, name="w2s", align_bytes=64)
        sT = const.tile([P, 8, 8, N_BLOCKS], F32, name="sT")
        b1t = const.tile([P, 2, 4], F32, name="b1t")
        b2t = const.tile([P, 8], F32, name="b2t")
        zall = const.tile([P, 640], BF16, name="zall")
        zf = const.tile([P, 640], F32, name="zf")

        def raw_tile():
            return r8.tile([P, 8, 512], BF16, tag="r8", name="raw", align_bytes=64)

        def load_bias():
            nc.vector.memset(zall[:], 0.0)
            nc.sync.dma_start(out=zall[0:2, 0:512], in_=b1.rearrange("(g x) -> g x", g=2))
            nc.sync.dma_start(
                out=zall[0:8, 512:640].rearrange("j (q b) -> j q b", q=4),
                in_=b2.rearrange("(q j b) -> j q b", q=4, j=8),
            )

        def load_objs(gq):
            raw = raw_tile()
            nc.sync.dma_start(
                out=raw[:].rearrange("p (s k) d -> p s (k d)", k=2),
                in_=obj_rows[512 * gq : 512 * (gq + 1), :].rearrange("(s p) d -> p s d", p=P),
            )
            return raw

        def load_w1(g, part):
            raw = raw_tile()
            nc.sync.dma_start(
                out=raw[:].rearrange("p (t k) d -> p t (k d)", k=2),
                in_=W1[512 * g : 512 * (g + 1), 1024 * part : 1024 * (part + 1)].rearrange("(m t) k -> m t k", t=4),
            )
            return raw

        def load_w2(kk):
            raw = raw_tile()
            nc.sync.dma_start(
                out=raw[:],
                in_=W2[:, 512 * kk : 512 * (kk + 1)].rearrange("(s m) g -> m s g", m=P),
            )
            return raw

        def prep_bias():
            nc.vector.tensor_copy(out=zf[:], in_=zall[:])
            pb1 = psum_tile([P, 4, P], "s1", "pb1")
            for t in range(4):
                nc.tensor.transpose(pb1[:, t, :], zf[:, t:512:4], ident[:])
            nc.vector.tensor_copy(out=b1t[:], in_=pb1[:, :, 0:2].rearrange("p t g -> p g t"))
            pb2 = psum_tile([P, 4, P], "s1", "pb2")
            nc.tensor.transpose(pb2[:, 0, :], zf[:, 512:640], ident[:])
            nc.vector.tensor_copy(out=b2t[:], in_=pb2[:, 0, 0:8])

        def turn_pair(raw, s0, in_head):
            words = raw[:].rearrange("p s k -> p (s k)").bitcast(F32)
            pt = head_psum(in_head)
            for s in range(2):
                for u in range(2):
                    base = (s0 + s) * 256
                    nc.tensor.transpose(pt[:, s, u, :], words[:, base + u : base + 256 : 2], ident[:])
            return pt

        def grp_tile():
            return mid.tile([P, 1024, 4], BF16, tag="mid8", name="grp", align_bytes=64)

        def plain_bank(raw, grp, sp, engine, in_head):
            gw = grp[:].rearrange("p c j -> p (c j)").bitcast(F32)
            pt = turn_pair(raw, 2 * sp, in_head)
            word_copy(
                engine,
                gw[:, 512 * sp : 512 * (sp + 1)].rearrange("p (s r u) -> p s r u", s=2, u=2),
                pt[:].rearrange("p s u r -> p s r u"),
            )

        def w2_bank(raw, grp, sp, engine):
            gw = grp[:].rearrange("p c j -> p (c j)").bitcast(F32).rearrange(
                "p (j q b u) -> p j q b u", j=8, q=4, b=32
            )
            pt = turn_pair(raw, 2 * sp, True)
            for sl in range(2):
                word_copy(
                    engine,
                    gw[:, 4 * sl : 4 * sl + 4, sp, :, :],
                    pt[:, sl, :, :].rearrange("p u (j b) -> p j b u", j=4),
                )

        def quant(grp, codes, scales):
            nc.vector.quantize_mx(
                out=codes.bitcast(FP8X4), scales=scales, in_=grp[:].rearrange("p c j -> p (c j)")
            )

        ocs = {}
        ab = {}
        hbs = {}
        hq = {}
        xts = {}

        def stage1_mm(u, pairs):
            oc, osc = ocs[u // 4]
            banks = []
            for part, g in pairs:
                ps = psum_tile([P, 4, P], "s1", "ps1")
                for t in range(4):
                    for kk in range(2):
                        nc.tensor.matmul_mx(
                            out=ps[:, t, :],
                            lhsT=w1c[:, g, part, t, kk, :].bitcast(FP8X4),
                            lhsT_scale=w1s[:, g, part, t, kk, :],
                            rhs=oc[:, u % 4, kk, :].bitcast(FP8X4),
                            rhs_scale=osc[:, u % 4, kk, :],
                            start=(kk == 0),
                            stop=(kk == 1),
                        )
                banks.append((part, g, ps))
            return (u, banks)

        def stage1_out(job, engine):
            u, banks = job
            for part, g, ps in banks:
                if (u, part) not in ab:
                    ab[(u, part)] = abp.tile([P, 2, P, 4], F32, tag="at" if part == 0 else "bt", name="abt")
                dst = ab[(u, part)]
                src = ps[:].rearrange("p t c -> p c t")
                if part == 0:
                    nc.vector.tensor_tensor(
                        out=dst[:, g],
                        in0=src,
                        in1=b1t[:, g, :].unsqueeze(1).to_broadcast([P, P, 4]),
                        op=ALU.add,
                    )
                elif engine == "v":
                    nc.vector.tensor_copy(out=dst[:, g], in_=src)
                else:
                    nc.scalar.copy(out=dst[:, g], in_=src)

        def h_piece(engine, n, hb, g, b0, b1):
            u, beta = divmod(n, 2)
            nb = b1 - b0
            cols = slice(beta * 64 + 8 * b0, beta * 64 + 8 * b1)
            engine.tensor_tensor(
                out=hb[:, 64 * b0 : 64 * b1, :].rearrange("p (b k m) t -> p b k m t", b=nb, k=8),
                in0=ab[(u, 0)][:, g, cols, :].rearrange("p (b m) t -> p b m t", b=nb).unsqueeze(2).to_broadcast([P, nb, 8, 8, 4]),
                in1=ab[(u, 1)][:, g, cols, :].rearrange("p (b k) t -> p b k t", b=nb).unsqueeze(3).to_broadcast([P, nb, 8, 8, 4]),
                op=ALU.add,
            )

        def h_open(n):
            hb0 = hbp.tile([P, 512, 4], BF16, tag="hb0", name="hb0", align_bytes=64)
            hb1 = hbp.tile([P, 512, 4], BF16, tag="hb1", name="hb1", align_bytes=64, bufs=1)
            hc = cod.tile([P, 1024], U32, tag="hc", name="hc", align_bytes=64)
            hs = cod.tile([P, 1024], U8, tag="hs", name="hs", align_bytes=64)
            hbs[n] = (hb0, hb1)
            hq[n] = (hc, hs)

        def h_relu(n, g):
            flat = hbs[n][g][:].rearrange("p c t -> p (c t)")
            nc.vector.tensor_scalar_max(out=flat, in0=flat, scalar1=0.0)

        def h_quant(n, g):
            hc, hs = hq[n]
            tok = slice(g * 512, (g + 1) * 512)
            nc.vector.quantize_mx(
                out=hc[:, tok].bitcast(FP8X4), scales=hs[:, tok], in_=hbs[n][g][:].rearrange("p c t -> p (c t)")
            )

        def h_all(n):
            h_open(n)
            h_piece(nc.gpsimd, n, hbs[n][1], 1, 0, 8)
            h_piece(nc.gpsimd, n, hbs[n][0], 0, 8 - G_SETS0, 8)
            h_piece(nc.vector, n, hbs[n][0], 0, 0, 8 - G_SETS0)
            h_relu(n, 1)
            h_relu(n, 0)
            h_quant(n, 1)
            h_quant(n, 0)

        def stage2_open(i):
            xv = xvp.tile([P, 8, 8, 32], F32, tag="xv", name="xv", align_bytes=64, bufs=3)
            xp = xvp.tile([P, 8, 4, 64], F32, tag="xp", name="xp", align_bytes=64)
            xts[i] = (xv, xp)

        def stage2(i, j):
            hc, hs = hq[i]
            xv, xp = xts[i]
            y = psum_tile([P, 512], "y", "y")
            wcol = slice(j * P, (j + 1) * P)
            for g in range(2):
                tok = slice(g * 512, (g + 1) * 512)
                nc.tensor.matmul_mx(
                    out=y[:],
                    lhsT=w2c[:, g, wcol].bitcast(FP8X4),
                    lhsT_scale=w2s[:, g, wcol],
                    rhs=hc[:, tok].bitcast(FP8X4),
                    rhs_scale=hs[:, tok],
                    start=(g == 0),
                    stop=(g == 1),
                )
            nc.scalar.activation(
                out=xv[:, 0 : 2 * WIDE, j, :],
                in_=y[:, 0 : 64 * WIDE].rearrange("p (s a) -> p s a", a=32),
                func=ACT.Relu,
                bias=b2t[:, j : j + 1],
                scale=1.0,
            )
            for b in range(WIDE, 8):
                src = y[:, 64 * b : 64 * (b + 1)]
                if b < 4:
                    dst = xv[:, 2 * b : 2 * b + 2, j, :]
                    src = src.rearrange("p (s a) -> p s a", a=32)
                else:
                    dst = xp[:, j, b - 4, :]
                nc.scalar.activation(
                    out=dst,
                    in_=src,
                    func=ACT.Relu,
                    bias=b2t[:, j : j + 1],
                    scale=1.0,
                    accum_out=sT[:, j, b, i : i + 1],
                )

        def wide_sums(i):
            xv = xts[i][0]
            for b in range(WIDE):
                nc.vector.tensor_reduce(
                    out=sT[:, :, b, i],
                    in_=xv[:, 2 * b : 2 * b + 2, :, :].rearrange("p s j a -> p j s a"),
                    axis=mybir.AxisListType.XY,
                    op=ALU.add,
                )

        def perm_copy(engine, dst_rows, tb, hh):
            word_copy(
                engine,
                dst_rows.rearrange("t (q j b) -> t q j b", q=4, j=8)[:, :, 4 * hh : 4 * hh + 4, :],
                tb[:].rearrange("t (j q b) -> t q j b", j=4, q=4),
            )

        def back_pe_turn(i, sb):
            xp = xts[i][1]
            banks = []
            for hh in range(2):
                tb = psum_tile([P, 512], "tr", "tb")
                for jj in range(4):
                    nc.tensor.transpose(
                        tb[:, jj * P : (jj + 1) * P],
                        xp[:, hh * 4 + jj, 2 * sb : 2 * sb + 2, :].rearrange("p b q -> p (b q)"),
                        ident[:],
                    )
                banks.append(tb)
            return (i, sb, banks)

        def back_pe_out(turned, engine):
            i, sb, banks = turned
            xs = xsp.tile([P, OUTC], F32, tag="xs", name="xs")
            for hh in range(2):
                perm_copy(engine, xs[:], banks[hh], hh)
            row = (8 * i + 4 + 2 * sb) * 64
            nc.sync.dma_start(out=xp_rows[row : row + P, :], in_=xs[:])

        def back_ve(i):
            xv = xts[i][0]
            vt = r8.tile([P, 2048], F32, tag="r8", name="vt", align_bytes=64)
            nc.vector.transpose(out=vt[:], in_=xv[:].rearrange("p s j a -> p (s j a)"))
            row = 8 * i * 64
            for q in range(4):
                nc.sync.dma_start(
                    out=xp_rows[row : row + 256, 256 * q : 256 * (q + 1)].rearrange("(s a) c -> a s c", a=32),
                    in_=vt[32 * q : 32 * (q + 1), :].rearrange("p (s c) -> p s c", s=8),
                )

        def sums_out(bq):
            so = xsp.tile([P, OUTC], F32, tag="xs", name="so")
            for hh in range(2):
                tb = psum_tile([P, 512], "tr", "tbs")
                for jj in range(4):
                    nc.tensor.transpose(
                        tb[:, jj * P : (jj + 1) * P],
                        sT[:, hh * 4 + jj, 4 * bq : 4 * bq + 4, :].rearrange("p b i -> p (b i)"),
                        ident[:],
                    )
                perm_copy("s" if hh == 0 else "v", so[:], tb, hh)
            by_b = out_1.rearrange("(i b) c -> b i c", b=8)
            for bl in range(4):
                nc.sync.dma_start(out=by_b[4 * bq + bl], in_=so[32 * bl : 32 * (bl + 1), :])

        def oc_tiles(gq):
            oc = ocp.tile([P, 4, 2, P], U32, tag="oc", name="oc", align_bytes=64)
            osc = ocp.tile([P, 4, 2, P], U8, tag="osc", name="osc", align_bytes=64)
            ocs[gq] = (oc, osc)

        def quant_objs(gq, grp):
            oc_tiles(gq)
            oc, osc = ocs[gq]
            quant(grp, oc[:].rearrange("p s k c -> p (s k c)"), osc[:].rearrange("p s k c -> p (s k c)"))

        def w1_chunk(g, part):
            grp = grp_tile()
            for sp in range(4):
                plain_bank(w1raw[(g, part)], grp, sp, "v" if (sp == 0 and g == 0) else "s", True)
            quant(
                grp,
                w1c[:, g, part].rearrange("p t k m -> p (t k m)"),
                w1s[:, g, part].rearrange("p t k m -> p (t k m)"),
            )

        def w2_chunk(kk):
            grp = grp_tile()
            for sp in range(4):
                w2_bank(w2raw[kk], grp, sp, "s")
            quant(grp, w2c[:, kk, :], w2s[:, kk, :])

        load_bias()
        oraw = {0: load_objs(0)}
        w1raw = {}
        for g in range(2):
            for part in range(2):
                w1raw[(g, part)] = load_w1(g, part)
        w2raw = [load_w2(0)]
        prep_bias()

        grp = grp_tile()
        for sp in range(4):
            plain_bank(oraw[0], grp, sp, "v" if sp == 0 else "s", True)
        quant_objs(0, grp)
        w2raw.append(load_w2(1))
        w1_chunk(0, 0)
        oraw[1] = load_objs(1)
        w1_chunk(0, 1)
        h_open(0)
        stage1_out(stage1_mm(0, [(0, 0), (1, 0)]), "s")
        h_piece(nc.vector, 0, hbs[0][0], 0, 0, 8)
        w1_chunk(1, 0)
        h_relu(0, 0)
        w1_chunk(1, 1)
        h_quant(0, 0)
        stage1_out(stage1_mm(0, [(0, 1), (1, 1)]), "s")
        h_piece(nc.vector, 0, hbs[0][1], 1, 0, 8)
        w2_chunk(0)
        h_relu(0, 1)
        w2_chunk(1)
        h_quant(0, 1)
        stage1_out(stage1_mm(1, [(0, 0), (1, 0)]), "s")
        stage1_out(stage1_mm(1, [(0, 1), (1, 1)]), "s")
        h_open(1)
        h_piece(nc.vector, 1, hbs[1][0], 0, 0, 8)
        h_piece(nc.vector, 1, hbs[1][1], 1, 0, 8)
        h_relu(1, 0)
        h_relu(1, 1)
        h_quant(1, 0)
        h_quant(1, 1)

        OBJ_STEPS = {0: [(1, 0), (1, 1)], 1: [(1, 2)], 2: [(1, 3)]}
        for gq in (2, 3):
            for sp in range(4):
                OBJ_STEPS[8 * gq - 10 + sp] = [(gq, sp)]
        ogrp = {}
        jobs = [stage1_mm(2, [(0, 0), (0, 1)])]
        quants = []
        waiting = []
        for i in range(N_BLOCKS):
            n = i + 2
            for job in jobs:
                stage1_out(job, "v")
            jobs = []
            for turned in waiting:
                back_pe_out(turned, "v")
            waiting = []
            if i >= 1:
                wide_sums(i - 1)
                back_ve(i - 1)
            for gq in quants:
                quant_objs(gq, ogrp[gq])
            quants = []
            if n < N_BLOCKS:
                h_all(n)
            stage2_open(i)
            for j in range(4):
                stage2(i, j)
            late = "v" if n >= N_BLOCKS else "s"
            if i >= 1:
                back_pe_out(back_pe_turn(i - 1, 0), late)
            for j in range(4, 8):
                stage2(i, j)
            if i % 2 == 1 and (i + 5) // 2 < N_UNITS:
                jobs.append(stage1_mm((i + 5) // 2, [(0, 0), (0, 1)]))
            if i % 2 == 0 and (i + 4) // 2 < N_UNITS:
                jobs.append(stage1_mm((i + 4) // 2, [(1, 0), (1, 1)]))
            if i >= 1:
                waiting.append(back_pe_turn(i - 1, 1))
            for gq, sp in OBJ_STEPS.get(i, []):
                if sp == 0:
                    ogrp[gq] = grp_tile()
                plain_bank(oraw[gq], ogrp[gq], sp, "s", False)
                if sp == 3:
                    quants.append(gq)
            if i == 2 or i == 10:
                oraw[i // 8 + 2] = load_objs(i // 8 + 2)
        last = N_BLOCKS - 1
        for turned in waiting:
            back_pe_out(turned, "v")
        wide_sums(last)
        back_ve(last)
        back_pe_out(back_pe_turn(last, 0), "s")
        back_pe_out(back_pe_turn(last, 1), "s")
        sums_out(0)
        sums_out(1)
